import numpy as np
import ml_dtypes


def mxq(x, axis, fmt="e4m3"):
    dtype, down = {"e4m3": (ml_dtypes.float8_e4m3fn, 7), "e5m2": (ml_dtypes.float8_e5m2, 14)}[fmt]
    v = np.moveaxis(np.asarray(x, np.float32).astype(ml_dtypes.bfloat16).astype(np.float64), axis, -1)
    blocks = v.reshape(v.shape[:-1] + (-1, 32))
    amax = np.abs(blocks).max(-1, keepdims=True)
    byte = np.maximum(np.where(amax > 0, np.frexp(amax)[1] - 1 + 127, 0) - down, 1)
    scale = np.exp2(byte - 127.0)
    codes = (blocks / scale).astype(np.float32).astype(dtype).astype(np.float64)
    return np.moveaxis((codes * scale).reshape(v.shape), -1, axis)


WIDE = False


def mx_kscale(k):
    if not WIDE:
        return np.ones(k)
    levels = np.array([10, -10, 5, -5, 0])
    a = np.random.permutation(np.resize(levels, k // 512 * 4)).reshape(k // 512, 4)
    idx = np.arange(k)
    return np.exp2(a[idx // 512, idx % 128 // 32])


BF16 = ml_dtypes.bfloat16


def bf(x):
    return np.asarray(x, np.float32).astype(BF16)


def f64(x):
    return np.asarray(x).astype(np.float64)


B, S, D, H, NS = 8, 512, 512, 4, 3
DH = D // H


def heads(x):
    return x.reshape(B, S, H, DH).transpose(0, 2, 1, 3)


def setup_inputs():
    s = mx_kscale(D)

    def stream():
        return bf(np.random.standard_normal((B, S, D)) * s)

    def weight():
        return bf(np.random.standard_normal((D, D)) / np.sqrt(D) / s[:, None])

    def bias():
        return bf(np.random.standard_normal(D) * 0.1)

    w = (0.4 + 0.3 * np.random.random((NS, NS))) * np.sign(np.random.standard_normal((NS, NS)))
    return {"input_tensor": stream(), "position_embedding": stream(), "attr": stream(),
            "Wq": weight(), "bq": bias(), "Wqp": weight(), "bqp": bias(), "Wqa": weight(), "bqa": bias(),
            "w_matrix": bf(w)}


def reference(input_tensor, position_embedding, attr, Wq, bq, Wqp, bqp, Wqa, bqa, w_matrix):
    Qi = heads((mxq(f64(input_tensor), 2, "e4m3") @ mxq(f64(Wq), 0, "e4m3")) + f64(bq))
    Qp = heads((mxq(f64(position_embedding), 2, "e4m3") @ mxq(f64(Wqp), 0, "e4m3")) + f64(bqp))
    Qa = heads((mxq(f64(attr), 2, "e4m3") @ mxq(f64(Wqa), 0, "e4m3")) + f64(bqa))
    w = f64(w_matrix)
    Q_ki = w[0, 0] * Qi + w[1, 0] * Qp + w[2, 0] * Qa
    Q_kp = w[0, 1] * Qi + w[1, 1] * Qp + w[2, 1] * Qa
    Q_ka = w[0, 2] * Qi + w[1, 2] * Qp + w[2, 2] * Qa
    return Q_ki, Q_kp, Q_ka

@@ -1,0 +1,223 @@
+from contextlib import ExitStack
+
+import concourse.mybir as mybir
+from concourse.masks import make_identity
+
+F32 = mybir.dt.float32
+BF16 = mybir.dt.bfloat16
+U32 = mybir.dt.uint32
+U8 = mybir.dt.uint8
+FP8X4 = mybir.dt.float8_e4m3fn_x4
+MULT = mybir.AluOpType.mult
+ADD = mybir.AluOpType.add
+COPY = mybir.ActivationFunctionType.Copy
+
+P = 128
+PACK = 4
+NB, S, D, H, NS = 8, 512, 512, 4, 3
+DH = D // H
+TILES = S // P
+WORDS = D // 2
+AHEAD = 3
+
+FLOPS = 2 * NS * NB * S * D * D
+
+
+def tile_crossmultiheadattention_pa_t_kernel(
+    tc,
+    input_tensor,
+    position_embedding,
+    attr,
+    Wq,
+    bq,
+    Wqp,
+    bqp,
+    Wqa,
+    bqa,
+    w_matrix,
+    out_0,
+    out_1,
+    out_2,
+):
+    nc = tc.nc
+    streams = (input_tensor, position_embedding, attr)
+    weights = (Wq, Wqp, Wqa)
+    biases = (bq, bqp, bqa)
+    outs = (out_0, out_1, out_2)
+
+    with ExitStack() as ctx:
+        const = ctx.enter_context(tc.tile_pool(name="const", bufs=1))
+        x_pool = ctx.enter_context(tc.tile_pool(name="x", bufs=AHEAD))
+        grouped_pool = ctx.enter_context(tc.tile_pool(name="grouped", bufs=NS))
+        mx_pool = ctx.enter_context(tc.tile_pool(name="mx", bufs=2))
+        first_pool = ctx.enter_context(tc.tile_pool(name="first", bufs=2 * NS))
+        out_pool = ctx.enter_context(tc.tile_pool(name="out", bufs=3))
+        psum = ctx.enter_context(tc.psum_pool(name="psum", bufs=2))
+
+        x_raw = {}
+        x_grouped = {}
+        x_codes = {}
+        x_scales = {}
+        acc = {}
+
+        def load_stream(b, i):
+            raw = x_pool.tile([P, TILES * D], BF16, tag="x%d" % i, name="x%d" % i)
+            nc.sync.dma_start(out=raw[:], in_=streams[i][b].rearrange("(p j) k -> p (j k)", j=TILES))
+            x_raw[(b, i)] = raw
+
+        def transpose_stream(b, i):
+            words = x_raw[(b, i)][:].bitcast(F32)
+            grouped = grouped_pool.tile([P, S * PACK], BF16, tag="grouped", name="grouped", align_bytes=64)
+            grouped_words = grouped[:].bitcast(F32)
+            for half in range(2):
+                xt = psum.tile([P, 4 * P], F32, tag="xt", name="xt")
+                for jj in range(2):
+                    for u in range(2):
+                        first_word = (2 * half + jj) * WORDS + u * P
+                        nc.tensor.transpose(
+                            out=xt[:, (2 * jj + u) * P : (2 * jj + u + 1) * P],
+                            in_=words[:, first_word : first_word + P],
+                            identity=ident[:],
+                        )
+                nc.scalar.copy(
+                    out=grouped_words[:, half * 4 * P : (half + 1) * 4 * P].rearrange(
+                        "q (jj r u) -> q jj r u", jj=2, u=2
+                    ),
+                    in_=xt[:].rearrange("q (jj u r) -> q jj r u", jj=2, u=2),
+                )
+            x_grouped[(b, i)] = grouped
+
+        def quantise_stream(b, i):
+            codes = mx_pool.tile([P, S], U32, tag="codes%d" % i, name="codes%d" % i, align_bytes=64)
+            scales = mx_pool.tile([P, S], U8, tag="scales%d" % i, name="scales%d" % i, align_bytes=64)
+            nc.vector.quantize_mx(out=codes[:].bitcast(FP8X4), scales=scales[:], in_=x_grouped[(b, i)][:])
+            x_codes[(b, i)] = codes
+            x_scales[(b, i)] = scales
+
+        def by_head(ap):
+            return ap.rearrange("p (h c) -> p h c", h=H)
+
+        def mix_tile(b, j):
+            tokens = slice(j * P, (j + 1) * P)
+            q = []
+            for i in range(NS):
+                q_i = psum.tile([P, D], F32, tag="q%d" % i, name="q%d" % i)
+                nc.tensor.matmul_mx(
+                    out=q_i[:],
+                    lhsT=x_codes[(b, i)][:, tokens].bitcast(FP8X4),
+                    lhsT_scale=x_scales[(b, i)][:, tokens],
+                    rhs=w_codes[i][:].bitcast(FP8X4),
+                    rhs_scale=w_scales[i][:],
+                    start=True,
+                    stop=True,
+                )
+                q.append(q_i)
+            first = []
+            for o in range(NS):
+                first_o = first_pool.tile([P, D], F32, tag="first", name="first")
+                nc.scalar.activation(out=first_o[:], in_=q[0][:], func=COPY, scale=w_all[:, o : o + 1])
+                first.append(first_o)
+            for o in range(NS):
+                nc.vector.scalar_tensor_tensor(
+                    out=acc[(b, o)][:, :, j, :],
+                    in0=by_head(q[1][:]),
+                    scalar=w_all[:, NS + o : NS + o + 1],
+                    in1=by_head(beta[o][:]),
+                    op0=MULT,
+                    op1=ADD,
+                )
+            for o in range(NS):
+                nc.vector.scalar_tensor_tensor(
+                    out=acc[(b, o)][:, :, j, :],
+                    in0=by_head(q[2][:]),
+                    scalar=w_all[:, 2 * NS + o : 2 * NS + o + 1],
+                    in1=acc[(b, o)][:, :, j, :],
+                    op0=MULT,
+                    op1=ADD,
+                )
+            for o in range(NS):
+                nc.gpsimd.tensor_tensor(
+                    out=acc[(b, o)][:, :, j, :],
+                    in0=acc[(b, o)][:, :, j, :],
+                    in1=by_head(first[o][:]),
+                    op=ADD,
+                )
+
+        ident = const.tile([P, P], F32, name="ident")
+        make_identity(nc, ident[:])
+
+        w_bf = const.tile([P, NS * NS], BF16, name="w_bf")
+        nc.scalar.dma_start(out=w_bf[:], in_=w_matrix.rearrange("i o -> (i o)").partition_broadcast(P))
+        w_all = const.tile([P, NS * NS], F32, name="w_all")
+        nc.vector.tensor_copy(out=w_all[:], in_=w_bf[:])
+
+        w_rows = const.tile([P, NS], BF16, name="w_rows")
+        nc.vector.memset(w_rows[:], 0.0)
+        nc.scalar.dma_start(out=w_rows[0:NS, :], in_=w_matrix)
+        bias_rows = const.tile([P, D], BF16, name="bias_rows")
+        nc.vector.memset(bias_rows[:], 0.0)
+        for i in range(NS):
+            nc.scalar.dma_start(out=bias_rows[i : i + 1, :], in_=biases[i].rearrange("(o c) -> o c", o=1))
+
+        w_raw = []
+        for i in range(NS):
+            raw = const.tile([P, PACK, D], BF16, name="w_raw%d" % i)
+            nc.sync.dma_start(
+                out=raw[:].rearrange("q (u e) n -> q u (e n)", u=2),
+                in_=weights[i].rearrange("(u q e) n -> q u (e n)", u=2, e=2),
+            )
+            w_raw.append(raw)
+            load_stream(0, i)
+        for b in range(1, AHEAD):
+            for i in range(NS):
+                load_stream(b, i)
+
+        w_codes = []
+        w_scales = []
+        for i in range(NS):
+            grouped = const.tile([P, D, PACK], BF16, name="w_grouped%d" % i, align_bytes=64)
+            nc.vector.tensor_copy(out=grouped[:], in_=w_raw[i][:].rearrange("q t n -> q n t"))
+            codes = const.tile([P, D], U32, name="w_codes%d" % i, align_bytes=64)
+            scales = const.tile([P, D], U8, name="w_scales%d" % i, align_bytes=64)
+            nc.vector.quantize_mx(
+                out=codes[:].bitcast(FP8X4), scales=scales[:], in_=grouped[:].rearrange("q n t -> q (n t)")
+            )
+            w_codes.append(codes)
+            w_scales.append(scales)
+
+        beta = []
+        for o in range(NS):
+            beta_ps = psum.tile([P, D], F32, tag="q%d" % o, name="beta_ps")
+            nc.tensor.matmul(
+                out=beta_ps[:],
+                lhsT=w_rows[:, o : o + 1].to_broadcast([P, P]),
+                rhs=bias_rows[:],
+                start=True,
+                stop=True,
+            )
+            beta_o = const.tile([P, D], F32, name="beta%d" % o)
+            nc.scalar.copy(out=beta_o[:], in_=beta_ps[:])
+            beta.append(beta_o)
+
+        for i in range(NS):
+            transpose_stream(0, i)
+        for i in range(NS):
+            quantise_stream(0, i)
+
+        for b in range(NB):
+            if b + AHEAD < NB:
+                for i in range(NS):
+                    load_stream(b + AHEAD, i)
+            for o in range(NS):
+                acc[(b, o)] = out_pool.tile([P, H, TILES, DH], F32, tag="out%d" % o, name="out%d" % o)
+            for j in range(TILES):
+                if b + 1 < NB and j < NS:
+                    transpose_stream(b + 1, j)
+                if b + 1 < NB and j >= 1:
+                    quantise_stream(b + 1, j - 1)
+                mix_tile(b, j)
+            for o in range(NS):
+                nc.sync.dma_start(
+                    out=outs[o][b].rearrange("h (p j) c -> p h (j c)", j=TILES),
+                    in_=acc[(b, o)][:].rearrange("p h j c -> p h (j c)"),
+                )

@@ -19,6 +19,9 @@ DH = D // H
 TILES = S // P
 WORDS = D // 2
 AHEAD = 3
+LEAD = 2
+HALVES = 2
+STORE_TILES = 2
 
 FLOPS = 2 * NS * NB * S * D * D
 
@@ -50,7 +53,6 @@ def tile_crossmultiheadattention_pa_t_kernel(
         x_pool = ctx.enter_context(tc.tile_pool(name="x", bufs=AHEAD))
         grouped_pool = ctx.enter_context(tc.tile_pool(name="grouped", bufs=NS))
         mx_pool = ctx.enter_context(tc.tile_pool(name="mx", bufs=2))
-        first_pool = ctx.enter_context(tc.tile_pool(name="first", bufs=2 * NS))
         out_pool = ctx.enter_context(tc.tile_pool(name="out", bufs=3))
         psum = ctx.enter_context(tc.psum_pool(name="psum", bufs=2))
 
@@ -65,27 +67,28 @@ def tile_crossmultiheadattention_pa_t_kernel(
             nc.sync.dma_start(out=raw[:], in_=streams[i][b].rearrange("(p j) k -> p (j k)", j=TILES))
             x_raw[(b, i)] = raw
 
-        def transpose_stream(b, i):
-            words = x_raw[(b, i)][:].bitcast(F32)
-            grouped = grouped_pool.tile([P, S * PACK], BF16, tag="grouped", name="grouped", align_bytes=64)
-            grouped_words = grouped[:].bitcast(F32)
-            for half in range(2):
-                xt = psum.tile([P, 4 * P], F32, tag="xt", name="xt")
-                for jj in range(2):
-                    for u in range(2):
-                        first_word = (2 * half + jj) * WORDS + u * P
-                        nc.tensor.transpose(
-                            out=xt[:, (2 * jj + u) * P : (2 * jj + u + 1) * P],
-                            in_=words[:, first_word : first_word + P],
-                            identity=ident[:],
-                        )
-                nc.scalar.copy(
-                    out=grouped_words[:, half * 4 * P : (half + 1) * 4 * P].rearrange(
-                        "q (jj r u) -> q jj r u", jj=2, u=2
-                    ),
-                    in_=xt[:].rearrange("q (jj u r) -> q jj r u", jj=2, u=2),
+        def transpose_half(b, i, half):
+            if half == 0:
+                x_grouped[(b, i)] = grouped_pool.tile(
+                    [P, S * PACK], BF16, tag="grouped", name="grouped", align_bytes=64
                 )
-            x_grouped[(b, i)] = grouped
+            words = x_raw[(b, i)][:].bitcast(F32)
+            grouped_words = x_grouped[(b, i)][:].bitcast(F32)
+            xt = psum.tile([P, 4 * P], F32, tag="xt", name="xt")
+            for jj in range(2):
+                for u in range(2):
+                    first_word = (2 * half + jj) * WORDS + u * P
+                    nc.tensor.transpose(
+                        out=xt[:, (2 * jj + u) * P : (2 * jj + u + 1) * P],
+                        in_=words[:, first_word : first_word + P],
+                        identity=ident[:],
+                    )
+            nc.scalar.copy(
+                out=grouped_words[:, half * 4 * P : (half + 1) * 4 * P].rearrange(
+                    "q (jj r u) -> q jj r u", jj=2, u=2
+                ),
+                in_=xt[:].rearrange("q (jj u r) -> q jj r u", jj=2, u=2),
+            )
 
         def quantise_stream(b, i):
             codes = mx_pool.tile([P, S], U32, tag="codes%d" % i, name="codes%d" % i, align_bytes=64)
@@ -97,51 +100,46 @@ def tile_crossmultiheadattention_pa_t_kernel(
         def by_head(ap):
             return ap.rearrange("p (h c) -> p h c", h=H)
 
-        def mix_tile(b, j):
+        def project(b, j, i):
             tokens = slice(j * P, (j + 1) * P)
-            q = []
-            for i in range(NS):
-                q_i = psum.tile([P, D], F32, tag="q%d" % i, name="q%d" % i)
-                nc.tensor.matmul_mx(
-                    out=q_i[:],
-                    lhsT=x_codes[(b, i)][:, tokens].bitcast(FP8X4),
-                    lhsT_scale=x_scales[(b, i)][:, tokens],
-                    rhs=w_codes[i][:].bitcast(FP8X4),
-                    rhs_scale=w_scales[i][:],
-                    start=True,
-                    stop=True,
-                )
-                q.append(q_i)
-            first = []
+            q_i = psum.tile([P, D], F32, tag="q%d" % i, name="q%d" % i)
+            nc.tensor.matmul_mx(
+                out=q_i[:],
+                lhsT=x_codes[(b, i)][:, tokens].bitcast(FP8X4),
+                lhsT_scale=x_scales[(b, i)][:, tokens],
+                rhs=w_codes[i][:].bitcast(FP8X4),
+                rhs_scale=w_scales[i][:],
+                start=True,
+                stop=True,
+            )
+            return by_head(q_i[:])
+
+        def first_part(t):
+            b, j = divmod(t, TILES)
+            if j == 0:
+                for o in range(NS):
+                    acc[(b, o)] = out_pool.tile([P, H, TILES, DH], F32, tag="out%d" % o, name="out%d" % o)
+            q_0 = project(b, j, 0)
             for o in range(NS):
-                first_o = first_pool.tile([P, D], F32, tag="first", name="first")
-                nc.scalar.activation(out=first_o[:], in_=q[0][:], func=COPY, scale=w_all[:, o : o + 1])
-                first.append(first_o)
-            for o in range(NS):
-                nc.vector.scalar_tensor_tensor(
-                    out=acc[(b, o)][:, :, j, :],
-                    in0=by_head(q[1][:]),
-                    scalar=w_all[:, NS + o : NS + o + 1],
-                    in1=by_head(beta[o][:]),
-                    op0=MULT,
-                    op1=ADD,
-                )
-            for o in range(NS):
-                nc.vector.scalar_tensor_tensor(
-                    out=acc[(b, o)][:, :, j, :],
-                    in0=by_head(q[2][:]),
-                    scalar=w_all[:, 2 * NS + o : 2 * NS + o + 1],
-                    in1=acc[(b, o)][:, :, j, :],
-                    op0=MULT,
-                    op1=ADD,
-                )
+                nc.scalar.activation(out=acc[(b, o)][:, :, j, :], in_=q_0, func=COPY, scale=w_all[:, o : o + 1])
             for o in range(NS):
                 nc.gpsimd.tensor_tensor(
-                    out=acc[(b, o)][:, :, j, :],
-                    in0=acc[(b, o)][:, :, j, :],
-                    in1=by_head(first[o][:]),
-                    op=ADD,
+                    out=acc[(b, o)][:, :, j, :], in0=acc[(b, o)][:, :, j, :], in1=by_head(beta[o][:]), op=ADD
                 )
+
+        def rest_part(t):
+            b, j = divmod(t, TILES)
+            for i in range(1, NS):
+                q_i = project(b, j, i)
+                for o in range(NS):
+                    nc.vector.scalar_tensor_tensor(
+                        out=acc[(b, o)][:, :, j, :],
+                        in0=q_i,
+                        scalar=w_all[:, NS * i + o : NS * i + o + 1],
+                        in1=acc[(b, o)][:, :, j, :],
+                        op0=MULT,
+                        op1=ADD,
+                    )
 
         ident = const.tile([P, P], F32, name="ident")
         make_identity(nc, ident[:])
@@ -172,19 +170,6 @@ def tile_crossmultiheadattention_pa_t_kernel(
             for i in range(NS):
                 load_stream(b, i)
 
-        w_codes = []
-        w_scales = []
-        for i in range(NS):
-            grouped = const.tile([P, D, PACK], BF16, name="w_grouped%d" % i, align_bytes=64)
-            nc.vector.tensor_copy(out=grouped[:], in_=w_raw[i][:].rearrange("q t n -> q n t"))
-            codes = const.tile([P, D], U32, name="w_codes%d" % i, align_bytes=64)
-            scales = const.tile([P, D], U8, name="w_scales%d" % i, align_bytes=64)
-            nc.vector.quantize_mx(
-                out=codes[:].bitcast(FP8X4), scales=scales[:], in_=grouped[:].rearrange("q n t -> q (n t)")
-            )
-            w_codes.append(codes)
-            w_scales.append(scales)
-
         beta = []
         for o in range(NS):
             beta_ps = psum.tile([P, D], F32, tag="q%d" % o, name="beta_ps")
@@ -199,25 +184,48 @@ def tile_crossmultiheadattention_pa_t_kernel(
             nc.scalar.copy(out=beta_o[:], in_=beta_ps[:])
             beta.append(beta_o)
 
-        for i in range(NS):
-            transpose_stream(0, i)
-        for i in range(NS):
+        w_codes = []
+        w_scales = []
+
+        def prepare_first_batch(i):
+            grouped = const.tile([P, D, PACK], BF16, name="w_grouped%d" % i, align_bytes=64)
+            nc.vector.tensor_copy(out=grouped[:], in_=w_raw[i][:].rearrange("q t n -> q n t"))
+            for half in range(HALVES):
+                transpose_half(0, i, half)
+            codes = const.tile([P, D], U32, name="w_codes%d" % i, align_bytes=64)
+            scales = const.tile([P, D], U8, name="w_scales%d" % i, align_bytes=64)
+            nc.vector.quantize_mx(
+                out=codes[:].bitcast(FP8X4), scales=scales[:], in_=grouped[:].rearrange("q n t -> q (n t)")
+            )
+            w_codes.append(codes)
+            w_scales.append(scales)
             quantise_stream(0, i)
 
-        for b in range(NB):
-            if b + AHEAD < NB:
+        prepare_first_batch(0)
+        for t in range(LEAD):
+            first_part(t)
+        for i in range(1, NS):
+            prepare_first_batch(i)
+
+        share = NS * HALVES // (TILES - LEAD)
+        for t in range(NB * TILES):
+            b, j = divmod(t, TILES)
+            if j == 0 and b + AHEAD < NB:
                 for i in range(NS):
                     load_stream(b + AHEAD, i)
-            for o in range(NS):
-                acc[(b, o)] = out_pool.tile([P, H, TILES, DH], F32, tag="out%d" % o, name="out%d" % o)
-            for j in range(TILES):
-                if b + 1 < NB and j < NS:
-                    transpose_stream(b + 1, j)
-                if b + 1 < NB and j >= 1:
-                    quantise_stream(b + 1, j - 1)
-                mix_tile(b, j)
-            for o in range(NS):
-                nc.sync.dma_start(
-                    out=outs[o][b].rearrange("h (p j) c -> p h (j c)", j=TILES),
-                    in_=acc[(b, o)][:].rearrange("p h j c -> p h (j c)"),
-                )
+            if b + 1 < NB and j == TILES - LEAD:
+                for i in range(NS):
+                    quantise_stream(b + 1, i)
+            if t + LEAD < NB * TILES:
+                first_part(t + LEAD)
+            rest_part(t)
+            if b + 1 < NB and j < TILES - LEAD:
+                for n in range(j * share, (j + 1) * share):
+                    transpose_half(b + 1, n // HALVES, n % HALVES)
+            if (j + 1) % STORE_TILES == 0:
+                done = slice(j + 1 - STORE_TILES, j + 1)
+                for o in range(NS):
+                    nc.sync.dma_start(
+                        out=outs[o][b].rearrange("h (p j) c -> p h j c", j=TILES)[:, :, done, :],
+                        in_=acc[(b, o)][:, :, done, :],
+                    )

@@ -19,9 +19,8 @@ DH = D // H
 TILES = S // P
 WORDS = D // 2
 AHEAD = 3
-LEAD = 2
-HALVES = 2
-STORE_TILES = 2
+VECTOR_ONLY_TILES = 3
+LAG_TILES = 4
 
 FLOPS = 2 * NS * NB * S * D * D
 
@@ -53,6 +52,7 @@ def tile_crossmultiheadattention_pa_t_kernel(
         x_pool = ctx.enter_context(tc.tile_pool(name="x", bufs=AHEAD))
         grouped_pool = ctx.enter_context(tc.tile_pool(name="grouped", bufs=NS))
         mx_pool = ctx.enter_context(tc.tile_pool(name="mx", bufs=2))
+        first_pool = ctx.enter_context(tc.tile_pool(name="first", bufs=LAG_TILES * NS))
         out_pool = ctx.enter_context(tc.tile_pool(name="out", bufs=3))
         psum = ctx.enter_context(tc.psum_pool(name="psum", bufs=2))
 
@@ -67,28 +67,27 @@ def tile_crossmultiheadattention_pa_t_kernel(
             nc.sync.dma_start(out=raw[:], in_=streams[i][b].rearrange("(p j) k -> p (j k)", j=TILES))
             x_raw[(b, i)] = raw
 
-        def transpose_half(b, i, half):
-            if half == 0:
-                x_grouped[(b, i)] = grouped_pool.tile(
-                    [P, S * PACK], BF16, tag="grouped", name="grouped", align_bytes=64
-                )
+        def transpose_stream(b, i):
             words = x_raw[(b, i)][:].bitcast(F32)
-            grouped_words = x_grouped[(b, i)][:].bitcast(F32)
-            xt = psum.tile([P, 4 * P], F32, tag="xt", name="xt")
-            for jj in range(2):
-                for u in range(2):
-                    first_word = (2 * half + jj) * WORDS + u * P
-                    nc.tensor.transpose(
-                        out=xt[:, (2 * jj + u) * P : (2 * jj + u + 1) * P],
-                        in_=words[:, first_word : first_word + P],
-                        identity=ident[:],
-                    )
-            nc.scalar.copy(
-                out=grouped_words[:, half * 4 * P : (half + 1) * 4 * P].rearrange(
-                    "q (jj r u) -> q jj r u", jj=2, u=2
-                ),
-                in_=xt[:].rearrange("q (jj u r) -> q jj r u", jj=2, u=2),
-            )
+            grouped = grouped_pool.tile([P, S * PACK], BF16, tag="grouped", name="grouped", align_bytes=64)
+            grouped_words = grouped[:].bitcast(F32)
+            for half in range(2):
+                xt = psum.tile([P, 4 * P], F32, tag="xt", name="xt")
+                for jj in range(2):
+                    for u in range(2):
+                        first_word = (2 * half + jj) * WORDS + u * P
+                        nc.tensor.transpose(
+                            out=xt[:, (2 * jj + u) * P : (2 * jj + u + 1) * P],
+                            in_=words[:, first_word : first_word + P],
+                            identity=ident[:],
+                        )
+                nc.scalar.copy(
+                    out=grouped_words[:, half * 4 * P : (half + 1) * 4 * P].rearrange(
+                        "q (jj r u) -> q jj r u", jj=2, u=2
+                    ),
+                    in_=xt[:].rearrange("q (jj u r) -> q jj r u", jj=2, u=2),
+                )
+            x_grouped[(b, i)] = grouped
 
         def quantise_stream(b, i):
             codes = mx_pool.tile([P, S], U32, tag="codes%d" % i, name="codes%d" % i, align_bytes=64)
@@ -100,45 +99,45 @@ def tile_crossmultiheadattention_pa_t_kernel(
         def by_head(ap):
             return ap.rearrange("p (h c) -> p h c", h=H)
 
-        def project(b, j, i):
+        def mix_tile(b, j):
             tokens = slice(j * P, (j + 1) * P)
-            q_i = psum.tile([P, D], F32, tag="q%d" % i, name="q%d" % i)
-            nc.tensor.matmul_mx(
-                out=q_i[:],
-                lhsT=x_codes[(b, i)][:, tokens].bitcast(FP8X4),
-                lhsT_scale=x_scales[(b, i)][:, tokens],
-                rhs=w_codes[i][:].bitcast(FP8X4),
-                rhs_scale=w_scales[i][:],
-                start=True,
-                stop=True,
-            )
-            return by_head(q_i[:])
-
-        def first_part(t):
-            b, j = divmod(t, TILES)
-            if j == 0:
-                for o in range(NS):
-                    acc[(b, o)] = out_pool.tile([P, H, TILES, DH], F32, tag="out%d" % o, name="out%d" % o)
-            q_0 = project(b, j, 0)
-            for o in range(NS):
-                nc.scalar.activation(out=acc[(b, o)][:, :, j, :], in_=q_0, func=COPY, scale=w_all[:, o : o + 1])
-            for o in range(NS):
-                nc.gpsimd.tensor_tensor(
-                    out=acc[(b, o)][:, :, j, :], in0=acc[(b, o)][:, :, j, :], in1=by_head(beta[o][:]), op=ADD
+            q = []
+            for i in range(NS):
+                q_i = psum.tile([P, D], F32, tag="q%d" % i, name="q%d" % i)
+                nc.tensor.matmul_mx(
+                    out=q_i[:],
+                    lhsT=x_codes[(b, i)][:, tokens].bitcast(FP8X4),
+                    lhsT_scale=x_scales[(b, i)][:, tokens],
+                    rhs=w_codes[i][:].bitcast(FP8X4),
+                    rhs_scale=w_scales[i][:],
+                    start=True,
+                    stop=True,
                 )
-
-        def rest_part(t):
-            b, j = divmod(t, TILES)
-            for i in range(1, NS):
-                q_i = project(b, j, i)
+                q.append(q_i)
+            vector_only = b * TILES + j >= NB * TILES - VECTOR_ONLY_TILES
+            vector_streams = (1, 2, 0) if vector_only else (1, 2)
+            for n, i in enumerate(vector_streams):
                 for o in range(NS):
                     nc.vector.scalar_tensor_tensor(
                         out=acc[(b, o)][:, :, j, :],
-                        in0=q_i,
+                        in0=by_head(q[i][:]),
                         scalar=w_all[:, NS * i + o : NS * i + o + 1],
-                        in1=acc[(b, o)][:, :, j, :],
+                        in1=by_head(beta[o][:]) if n == 0 else acc[(b, o)][:, :, j, :],
                         op0=MULT,
                         op1=ADD,
+                    )
+            if not vector_only:
+                first = []
+                for o in range(NS):
+                    first_o = first_pool.tile([P, D], F32, tag="first", name="first")
+                    nc.scalar.activation(out=first_o[:], in_=q[0][:], func=COPY, scale=w_all[:, o : o + 1])
+                    first.append(first_o)
+                for o in range(NS):
+                    nc.gpsimd.tensor_tensor(
+                        out=acc[(b, o)][:, :, j, :],
+                        in0=acc[(b, o)][:, :, j, :],
+                        in1=by_head(first[o][:]),
+                        op=ADD,
                     )
 
         ident = const.tile([P, P], F32, name="ident")
@@ -170,6 +169,19 @@ def tile_crossmultiheadattention_pa_t_kernel(
             for i in range(NS):
                 load_stream(b, i)
 
+        w_codes = []
+        w_scales = []
+        for i in range(NS):
+            grouped = const.tile([P, D, PACK], BF16, name="w_grouped%d" % i, align_bytes=64)
+            nc.vector.tensor_copy(out=grouped[:], in_=w_raw[i][:].rearrange("q t n -> q n t"))
+            codes = const.tile([P, D], U32, name="w_codes%d" % i, align_bytes=64)
+            scales = const.tile([P, D], U8, name="w_scales%d" % i, align_bytes=64)
+            nc.vector.quantize_mx(
+                out=codes[:].bitcast(FP8X4), scales=scales[:], in_=grouped[:].rearrange("q n t -> q (n t)")
+            )
+            w_codes.append(codes)
+            w_scales.append(scales)
+
         beta = []
         for o in range(NS):
             beta_ps = psum.tile([P, D], F32, tag="q%d" % o, name="beta_ps")
@@ -184,48 +196,25 @@ def tile_crossmultiheadattention_pa_t_kernel(
             nc.scalar.copy(out=beta_o[:], in_=beta_ps[:])
             beta.append(beta_o)
 
-        w_codes = []
-        w_scales = []
-
-        def prepare_first_batch(i):
-            grouped = const.tile([P, D, PACK], BF16, name="w_grouped%d" % i, align_bytes=64)
-            nc.vector.tensor_copy(out=grouped[:], in_=w_raw[i][:].rearrange("q t n -> q n t"))
-            for half in range(HALVES):
-                transpose_half(0, i, half)
-            codes = const.tile([P, D], U32, name="w_codes%d" % i, align_bytes=64)
-            scales = const.tile([P, D], U8, name="w_scales%d" % i, align_bytes=64)
-            nc.vector.quantize_mx(
-                out=codes[:].bitcast(FP8X4), scales=scales[:], in_=grouped[:].rearrange("q n t -> q (n t)")
-            )
-            w_codes.append(codes)
-            w_scales.append(scales)
+        for i in range(NS):
+            transpose_stream(0, i)
+        for i in range(NS):
             quantise_stream(0, i)
 
-        prepare_first_batch(0)
-        for t in range(LEAD):
-            first_part(t)
-        for i in range(1, NS):
-            prepare_first_batch(i)
-
-        share = NS * HALVES // (TILES - LEAD)
-        for t in range(NB * TILES):
-            b, j = divmod(t, TILES)
-            if j == 0 and b + AHEAD < NB:
+        for b in range(NB):
+            if b + AHEAD < NB:
                 for i in range(NS):
                     load_stream(b + AHEAD, i)
-            if b + 1 < NB and j == TILES - LEAD:
-                for i in range(NS):
-                    quantise_stream(b + 1, i)
-            if t + LEAD < NB * TILES:
-                first_part(t + LEAD)
-            rest_part(t)
-            if b + 1 < NB and j < TILES - LEAD:
-                for n in range(j * share, (j + 1) * share):
-                    transpose_half(b + 1, n // HALVES, n % HALVES)
-            if (j + 1) % STORE_TILES == 0:
-                done = slice(j + 1 - STORE_TILES, j + 1)
-                for o in range(NS):
-                    nc.sync.dma_start(
-                        out=outs[o][b].rearrange("h (p j) c -> p h j c", j=TILES)[:, :, done, :],
-                        in_=acc[(b, o)][:, :, done, :],
-                    )
+            for o in range(NS):
+                acc[(b, o)] = out_pool.tile([P, H, TILES, DH], F32, tag="out%d" % o, name="out%d" % o)
+            for j in range(TILES):
+                if b + 1 < NB and j < NS:
+                    transpose_stream(b + 1, j)
+                if b + 1 < NB and j >= 1:
+                    quantise_stream(b + 1, j - 1)
+                mix_tile(b, j)
+            for o in range(NS):
+                nc.sync.dma_start(
+                    out=outs[o][b].rearrange("h (p j) c -> p h (j c)", j=TILES),
+                    in_=acc[(b, o)][:].rearrange("p h j c -> p h (j c)"),
+                )

from contextlib import ExitStack

import concourse.mybir as mybir
from concourse.masks import make_identity

F32 = mybir.dt.float32
BF16 = mybir.dt.bfloat16
U32 = mybir.dt.uint32
U8 = mybir.dt.uint8
FP8X4 = mybir.dt.float8_e4m3fn_x4
MULT = mybir.AluOpType.mult
ADD = mybir.AluOpType.add
COPY = mybir.ActivationFunctionType.Copy

P = 128
PACK = 4
NB, S, D, H, NS = 8, 512, 512, 4, 3
DH = D // H
TILES = S // P
WORDS = D // 2
AHEAD = 3
VECTOR_ONLY_TILES = 3
LAG_TILES = 4

FLOPS = 2 * NS * NB * S * D * D


def tile_crossmultiheadattention_pa_t_kernel(
    tc,
    input_tensor,
    position_embedding,
    attr,
    Wq,
    bq,
    Wqp,
    bqp,
    Wqa,
    bqa,
    w_matrix,
    out_0,
    out_1,
    out_2,
):
    nc = tc.nc
    streams = (input_tensor, position_embedding, attr)
    weights = (Wq, Wqp, Wqa)
    biases = (bq, bqp, bqa)
    outs = (out_0, out_1, out_2)

    with ExitStack() as ctx:
        const = ctx.enter_context(tc.tile_pool(name="const", bufs=1))
        x_pool = ctx.enter_context(tc.tile_pool(name="x", bufs=AHEAD))
        grouped_pool = ctx.enter_context(tc.tile_pool(name="grouped", bufs=NS))
        mx_pool = ctx.enter_context(tc.tile_pool(name="mx", bufs=2))
        first_pool = ctx.enter_context(tc.tile_pool(name="first", bufs=LAG_TILES * NS))
        out_pool = ctx.enter_context(tc.tile_pool(name="out", bufs=3))
        psum = ctx.enter_context(tc.psum_pool(name="psum", bufs=2))

        x_raw = {}
        x_grouped = {}
        x_codes = {}
        x_scales = {}
        acc = {}

        def load_stream(b, i):
            raw = x_pool.tile([P, TILES * D], BF16, tag="x%d" % i, name="x%d" % i)
            nc.sync.dma_start(out=raw[:], in_=streams[i][b].rearrange("(p j) k -> p (j k)", j=TILES))
            x_raw[(b, i)] = raw

        def transpose_stream(b, i):
            words = x_raw[(b, i)][:].bitcast(F32)
            grouped = grouped_pool.tile([P, S * PACK], BF16, tag="grouped", name="grouped", align_bytes=64)
            grouped_words = grouped[:].bitcast(F32)
            for half in range(2):
                xt = psum.tile([P, 4 * P], F32, tag="xt", name="xt")
                for jj in range(2):
                    for u in range(2):
                        first_word = (2 * half + jj) * WORDS + u * P
                        nc.tensor.transpose(
                            out=xt[:, (2 * jj + u) * P : (2 * jj + u + 1) * P],
                            in_=words[:, first_word : first_word + P],
                            identity=ident[:],
                        )
                nc.scalar.copy(
                    out=grouped_words[:, half * 4 * P : (half + 1) * 4 * P].rearrange(
                        "q (jj r u) -> q jj r u", jj=2, u=2
                    ),
                    in_=xt[:].rearrange("q (jj u r) -> q jj r u", jj=2, u=2),
                )
            x_grouped[(b, i)] = grouped

        def quantise_stream(b, i):
            codes = mx_pool.tile([P, S], U32, tag="codes%d" % i, name="codes%d" % i, align_bytes=64)
            scales = mx_pool.tile([P, S], U8, tag="scales%d" % i, name="scales%d" % i, align_bytes=64)
            nc.vector.quantize_mx(out=codes[:].bitcast(FP8X4), scales=scales[:], in_=x_grouped[(b, i)][:])
            x_codes[(b, i)] = codes
            x_scales[(b, i)] = scales

        def by_head(ap):
            return ap.rearrange("p (h c) -> p h c", h=H)

        def mix_tile(b, j):
            tokens = slice(j * P, (j + 1) * P)
            q = []
            for i in range(NS):
                q_i = psum.tile([P, D], F32, tag="q%d" % i, name="q%d" % i)
                nc.tensor.matmul_mx(
                    out=q_i[:],
                    lhsT=x_codes[(b, i)][:, tokens].bitcast(FP8X4),
                    lhsT_scale=x_scales[(b, i)][:, tokens],
                    rhs=w_codes[i][:].bitcast(FP8X4),
                    rhs_scale=w_scales[i][:],
                    start=True,
                    stop=True,
                )
                q.append(q_i)
            vector_only = b * TILES + j >= NB * TILES - VECTOR_ONLY_TILES
            vector_streams = (1, 2, 0) if vector_only else (1, 2)
            for n, i in enumerate(vector_streams):
                for o in range(NS):
                    nc.vector.scalar_tensor_tensor(
                        out=acc[(b, o)][:, :, j, :],
                        in0=by_head(q[i][:]),
                        scalar=w_all[:, NS * i + o : NS * i + o + 1],
                        in1=by_head(beta[o][:]) if n == 0 else acc[(b, o)][:, :, j, :],
                        op0=MULT,
                        op1=ADD,
                    )
            if not vector_only:
                first = []
                for o in range(NS):
                    first_o = first_pool.tile([P, D], F32, tag="first", name="first")
                    nc.scalar.activation(out=first_o[:], in_=q[0][:], func=COPY, scale=w_all[:, o : o + 1])
                    first.append(first_o)
                for o in range(NS):
                    nc.gpsimd.tensor_tensor(
                        out=acc[(b, o)][:, :, j, :],
                        in0=acc[(b, o)][:, :, j, :],
                        in1=by_head(first[o][:]),
                        op=ADD,
                    )

        ident = const.tile([P, P], F32, name="ident")
        make_identity(nc, ident[:])

        w_bf = const.tile([P, NS * NS], BF16, name="w_bf")
        nc.scalar.dma_start(out=w_bf[:], in_=w_matrix.rearrange("i o -> (i o)").partition_broadcast(P))
        w_all = const.tile([P, NS * NS], F32, name="w_all")
        nc.vector.tensor_copy(out=w_all[:], in_=w_bf[:])

        w_rows = const.tile([P, NS], BF16, name="w_rows")
        nc.vector.memset(w_rows[:], 0.0)
        nc.scalar.dma_start(out=w_rows[0:NS, :], in_=w_matrix)
        bias_rows = const.tile([P, D], BF16, name="bias_rows")
        nc.vector.memset(bias_rows[:], 0.0)
        for i in range(NS):
            nc.scalar.dma_start(out=bias_rows[i : i + 1, :], in_=biases[i].rearrange("(o c) -> o c", o=1))

        w_raw = []
        for i in range(NS):
            raw = const.tile([P, PACK, D], BF16, name="w_raw%d" % i)
            nc.sync.dma_start(
                out=raw[:].rearrange("q (u e) n -> q u (e n)", u=2),
                in_=weights[i].rearrange("(u q e) n -> q u (e n)", u=2, e=2),
            )
            w_raw.append(raw)
            load_stream(0, i)
        for b in range(1, AHEAD):
            for i in range(NS):
                load_stream(b, i)

        w_codes = []
        w_scales = []
        for i in range(NS):
            grouped = const.tile([P, D, PACK], BF16, name="w_grouped%d" % i, align_bytes=64)
            nc.vector.tensor_copy(out=grouped[:], in_=w_raw[i][:].rearrange("q t n -> q n t"))
            codes = const.tile([P, D], U32, name="w_codes%d" % i, align_bytes=64)
            scales = const.tile([P, D], U8, name="w_scales%d" % i, align_bytes=64)
            nc.vector.quantize_mx(
                out=codes[:].bitcast(FP8X4), scales=scales[:], in_=grouped[:].rearrange("q n t -> q (n t)")
            )
            w_codes.append(codes)
            w_scales.append(scales)

        beta = []
        for o in range(NS):
            beta_ps = psum.tile([P, D], F32, tag="q%d" % o, name="beta_ps")
            nc.tensor.matmul(
                out=beta_ps[:],
                lhsT=w_rows[:, o : o + 1].to_broadcast([P, P]),
                rhs=bias_rows[:],
                start=True,
                stop=True,
            )
            beta_o = const.tile([P, D], F32, name="beta%d" % o)
            nc.scalar.copy(out=beta_o[:], in_=beta_ps[:])
            beta.append(beta_o)

        for i in range(NS):
            transpose_stream(0, i)
        for i in range(NS):
            quantise_stream(0, i)

        for b in range(NB):
            if b + AHEAD < NB:
                for i in range(NS):
                    load_stream(b + AHEAD, i)
            for o in range(NS):
                acc[(b, o)] = out_pool.tile([P, H, TILES, DH], F32, tag="out%d" % o, name="out%d" % o)
            for j in range(TILES):
                if b + 1 < NB and j < NS:
                    transpose_stream(b + 1, j)
                if b + 1 < NB and j >= 1:
                    quantise_stream(b + 1, j - 1)
                mix_tile(b, j)
            for o in range(NS):
                nc.sync.dma_start(
                    out=outs[o][b].rearrange("h (p j) c -> p h (j c)", j=TILES),
                    in_=acc[(b, o)][:].rearrange("p h j c -> p h (j c)"),
                )
